import numpy as np
import ml_dtypes


def mxq(x, axis, fmt="e4m3"):
    dtype, down = {"e4m3": (ml_dtypes.float8_e4m3fn, 7), "e5m2": (ml_dtypes.float8_e5m2, 14)}[fmt]
    v = np.moveaxis(np.asarray(x, np.float32).astype(ml_dtypes.bfloat16).astype(np.float64), axis, -1)
    blocks = v.reshape(v.shape[:-1] + (-1, 32))
    amax = np.abs(blocks).max(-1, keepdims=True)
    byte = np.maximum(np.where(amax > 0, np.frexp(amax)[1] - 1 + 127, 0) - down, 1)
    scale = np.exp2(byte - 127.0)
    codes = (blocks / scale).astype(np.float32).astype(dtype).astype(np.float64)
    return np.moveaxis((codes * scale).reshape(v.shape), -1, axis)


WIDE = False


def mx_kscale(k):
    if not WIDE:
        return np.ones(k)
    levels = np.array([10, -10, 5, -5, 0])
    if k % 512:
        return np.exp2(np.random.permutation(np.resize(levels, k // 32))).repeat(32)
    a = np.empty((k // 512, 16))
    for p in range(k // 512):
        a[p, :8] = np.random.permutation(np.resize(levels, 8))
        for g in range(8):
            far = levels[np.abs(levels - a[p, g]) >= 10]
            a[p, g + 8] = far[np.random.randint(len(far))]
    return np.exp2(a.ravel()).repeat(32)


BF16 = ml_dtypes.bfloat16


def bf(x):
    return np.asarray(x, np.float32).astype(BF16)


def f64(x):
    return np.asarray(x).astype(np.float64)


B, L, A, W = 128, 512, 2048, 8
EPS = 1e-8


def sigmoid(v):
    return 1.0 / (1.0 + np.exp(-v))


def setup_inputs():
    s, t = mx_kscale(L), mx_kscale(A)
    return {
        "z_current": bf(np.random.standard_normal((B, L)) * s),
        "z_window": bf(np.random.standard_normal((W, B, L)) * s),
        "Wq": bf(np.random.standard_normal((A, L)) / np.sqrt(L) / s),
        "Wk": bf(np.random.standard_normal((A, L)) / np.sqrt(L) / s),
        "Wv": bf(np.random.standard_normal((A, L)) / np.sqrt(L) / s * t[:, None]),
        "Wo": bf(np.random.standard_normal((L, A)) * 2.0 / np.sqrt(A) / t),
    }


def reference(z_current, z_window, Wq, Wk, Wv, Wo):
    sig_q = sigmoid(mxq(f64(z_current), 1, "e4m3") @ mxq(f64(Wq), 1, "e4m3").T)
    zw = mxq(f64(z_window), 2, "e4m3")
    k = zw @ mxq(f64(Wk), 1, "e4m3").T
    v = zw @ mxq(f64(Wv), 1, "e4m3").T
    m = k.max(axis=(1, 2), keepdims=True)
    e = np.exp(k - m)
    num = (e * v).sum(0)
    den = EPS + e.sum(0)
    h = sig_q * (num / den)
    return mxq(h, 1, "e4m3") @ mxq(f64(Wo), 1, "e4m3").T

@@ -1,0 +1,297 @@
+from contextlib import ExitStack
+
+import concourse.mybir as mybir
+from concourse.masks import make_identity
+
+F32 = mybir.dt.float32
+BF16 = mybir.dt.bfloat16
+U32 = mybir.dt.uint32
+U8 = mybir.dt.uint8
+FP8X4 = mybir.dt.float8_e4m3fn_x4
+ALU = mybir.AluOpType
+ACT = mybir.ActivationFunctionType
+AXIS_X = mybir.AxisListType.X
+
+P = 128
+L = 512
+A = 2048
+W = 8
+EPS = 1e-8
+CHUNK = 512
+CHUNKS = A // CHUNK
+BLOCKS = CHUNK // P
+WORDS = L // 2
+GROUP = 4
+ROUND = 2
+RUN = 4
+GPSIMD_STEPS = 6
+
+FLOPS = 2 * P * L * A * (1 + 2 * W) + 2 * P * A * L
+
+
+def tile_aftblock_pa_kernel(tc, z_current, z_window, Wq, Wk, Wv, Wo, out):
+    nc = tc.nc
+    with ExitStack() as ctx:
+        ctx.enter_context(tc.manual_schedule())
+        keep = ctx.enter_context(tc.tile_pool(name="keep", bufs=1))
+        stage = ctx.enter_context(tc.tile_pool(name="stage", bufs=6))
+        banks = ctx.enter_context(tc.psum_pool(name="banks", bufs=4))
+
+        ident = keep.tile([P, P], F32, name="ident")
+        make_identity(nc, ident[:])
+
+        z_codes = keep.tile([P, (W + 1) * P], U32, name="z_codes", align_bytes=64)
+        z_scales = keep.tile([P, (W + 1) * P], U8, name="z_scales", align_bytes=64)
+        wk_codes = keep.tile([P, A], U32, name="wk_codes", align_bytes=64)
+        wk_scales = keep.tile([P, A], U8, name="wk_scales", align_bytes=64)
+        wv_codes = keep.tile([P, A], U32, name="wv_codes", align_bytes=64)
+        wv_scales = keep.tile([P, A], U8, name="wv_scales", align_bytes=64)
+        wq_codes = keep.tile([P, A], U32, name="wq_codes", align_bytes=64)
+        wq_scales = keep.tile([P, A], U8, name="wq_scales", align_bytes=64)
+        wo_codes = keep.tile([P, CHUNKS * L], U32, name="wo_codes", align_bytes=64)
+        wo_scales = keep.tile([P, CHUNKS * L], U8, name="wo_scales", align_bytes=64)
+
+        k_sb = keep.tile([P, CHUNKS, W, CHUNK], F32, name="k_sb")
+        bank_max = keep.tile([P, CHUNKS, W], F32, name="bank_max")
+        row_max = keep.tile([P, W], F32, name="row_max")
+        neg_m = keep.tile([P, W], F32, name="neg_m")
+        gate = keep.tile([P, CHUNKS, P, BLOCKS], F32, name="gate")
+
+        def mx_pass(acc, lhs_codes, lhs_scales, lhs_cols, rhs_codes, rhs_scales, rhs_cols, start, stop):
+            nc.tensor.matmul_mx(
+                out=acc,
+                lhsT=lhs_codes[:, lhs_cols].bitcast(FP8X4),
+                lhsT_scale=lhs_scales[:, lhs_cols],
+                rhs=rhs_codes[:, rhs_cols].bitcast(FP8X4),
+                rhs_scale=rhs_scales[:, rhs_cols],
+                start=start,
+                stop=stop,
+            )
+
+        def step_cols(w):
+            return slice(w * P, (w + 1) * P)
+
+        def chunk_cols(c):
+            return slice(c * CHUNK, (c + 1) * CHUNK)
+
+        with tc.tile_pool(name="raw", bufs=1) as raw, tc.psum_pool(name="flip", bufs=4) as flip:
+            z_raw = raw.tile([P, W + 1, L], BF16, name="z_raw")
+            wk_raw = raw.tile([P, A // P, L], BF16, name="wk_raw")
+            wv_raw = raw.tile([P, A // P, L], BF16, name="wv_raw")
+            wq_raw = raw.tile([P, A // P, L], BF16, name="wq_raw")
+            wo_raw = raw.tile([P, L // P, A], BF16, name="wo_raw")
+
+            def load_steps(first):
+                steps = slice(first, first + GROUP)
+                nc.sync.dma_start(out=z_raw[:, steps, :], in_=z_window[steps].rearrange("w b l -> b w l"))
+
+            def load_features(tile_, weight, c):
+                rows = weight.rearrange("(c r t) l -> r c t l", c=CHUNKS, t=BLOCKS)
+                nc.sync.dma_start(out=tile_[:, BLOCKS * c : BLOCKS * (c + 1), :], in_=rows[:, c])
+
+            def load_wo(g):
+                nc.sync.dma_start(out=wo_raw[:, :, chunk_cols(g)], in_=Wo.rearrange("(i p) a -> p i a", p=P)[:, :, chunk_cols(g)])
+
+            load_steps(0)
+            load_features(wk_raw, Wk, 0)
+            nc.sync.dma_start(out=z_raw[:, W, :], in_=z_current)
+            load_steps(GROUP)
+            for c in range(1, CHUNKS):
+                load_features(wk_raw, Wk, c)
+            for c in range(CHUNKS):
+                load_features(wq_raw, Wq, c)
+            for c in range(CHUNKS):
+                load_features(wv_raw, Wv, c)
+            for g in range(CHUNKS):
+                load_wo(g)
+
+            def transpose_group(blocks, share_with_vector):
+                grouped = stage.tile([P, len(blocks) * P * BLOCKS], BF16, name="grouped", align_bytes=64)
+                words = grouped[:].bitcast(F32).rearrange("p (k r u) -> p k r u", r=P, u=2)
+                for first in range(0, len(blocks), 2):
+                    pair = blocks[first : first + 2]
+                    flipped = flip.tile([P, 2, 2, P], F32, name="flipped")
+                    for k, block in enumerate(pair):
+                        for u in range(2):
+                            nc.tensor.transpose(flipped[:, k, u, :], block[:, u : WORDS : 2], ident[:])
+                    source = flipped[:, 0 : len(pair)].rearrange("p k u r -> p k r u")
+                    target = words[:, first : first + len(pair)]
+                    if share_with_vector and first > 0:
+                        nc.vector.tensor_copy(out=target, in_=source)
+                    else:
+                        nc.scalar.copy(out=target, in_=source)
+                return grouped
+
+            def quantise(grouped, codes, scales):
+                nc.vector.quantize_mx(out=codes.bitcast(FP8X4), scales=scales, in_=grouped[:])
+
+            def group_of(blocks, codes, scales, i):
+                cols = slice(GROUP * P * i, GROUP * P * (i + 1))
+                return blocks[GROUP * i : GROUP * (i + 1)], codes[:, cols], scales[:, cols]
+
+            z_blocks = [z_raw[:, s, :].bitcast(F32) for s in range(W + 1)]
+            wk_blocks = [wk_raw[:, j, :].bitcast(F32) for j in range(A // P)]
+            wv_blocks = [wv_raw[:, j, :].bitcast(F32) for j in range(A // P)]
+            wq_blocks = [wq_raw[:, j, :].bitcast(F32) for j in range(A // P)]
+            wo_blocks = [
+                wo_raw[:, i, :].bitcast(F32)[:, WORDS * g : WORDS * (g + 1)]
+                for g in range(CHUNKS)
+                for i in range(L // P)
+            ]
+
+            for blocks, codes, scales in (group_of(z_blocks, z_codes, z_scales, 0), group_of(wk_blocks, wk_codes, wk_scales, 0)):
+                quantise(transpose_group(blocks, True), codes, scales)
+            waiting = (transpose_group(z_blocks[W:], False), z_codes[:, W * P :], z_scales[:, W * P :])
+
+            later = (
+                [group_of(z_blocks, z_codes, z_scales, 1)]
+                + [group_of(wk_blocks, wk_codes, wk_scales, c) for c in range(1, CHUNKS)]
+                + [group_of(wq_blocks, wq_codes, wq_scales, c) for c in range(CHUNKS)]
+                + [group_of(wv_blocks, wv_codes, wv_scales, c) for c in range(CHUNKS)]
+            )
+            last = [group_of(wo_blocks, wo_codes, wo_scales, g) for g in range(CHUNKS)]
+            gate_round = len(later) - CHUNKS + 2
+
+            def gate_stage():
+                for c in range(CHUNKS):
+                    q_ps = flip.tile([P, BLOCKS, P], F32, name="q_ps", tag="flipped")
+                    for t in range(BLOCKS):
+                        mx_pass(q_ps[:, t, :], wq_codes, wq_scales, step_cols(BLOCKS * c + t),
+                                z_codes, z_scales, step_cols(W), True, True)
+                    nc.scalar.activation(out=gate[:, c], in_=q_ps[:].rearrange("p t b -> p b t"), func=ACT.Exp, scale=-1.0)
+                flat = gate[:].rearrange("p c b t -> p (c b t)")
+                nc.gpsimd.tensor_scalar(out=flat, in0=flat, scalar1=1.0, scalar2=1.0, op0=ALU.add, op1=ALU.mult)
+
+            def row_maxima(first):
+                steps = slice(first, first + BLOCKS)
+                nc.vector.tensor_reduce(
+                    out=row_max[:, steps], in_=bank_max[:, :, steps].rearrange("p c w -> p w c"), axis=AXIS_X, op=ALU.max
+                )
+
+            def spread_maxima(first):
+                spread = banks.tile([P, BLOCKS, P], F32, name="spread", tag="bank")
+                for i in range(BLOCKS):
+                    nc.tensor.transpose(spread[:, i, :], row_max[:, first + i : first + i + 1].to_broadcast([P, P]), ident[:])
+                return spread
+
+            def negated_maximum(spread, first):
+                nc.vector.tensor_reduce(out=neg_m[:, first : first + BLOCKS], in_=spread[:], axis=AXIS_X, op=ALU.max, negate=True)
+
+            first_steps = 0
+            last_steps = BLOCKS
+            wo_grouped = []
+            rounds = CHUNKS * W // ROUND
+            for round_ in range(rounds):
+                for bank in range(ROUND * round_, ROUND * (round_ + 1)):
+                    c, w = divmod(bank, W)
+                    k_ps = banks.tile([P, CHUNK], F32, name="k_ps", tag="bank")
+                    mx_pass(k_ps[:], z_codes, z_scales, step_cols(w), wk_codes, wk_scales, chunk_cols(c), True, True)
+                    nc.vector.tensor_scalar(
+                        out=k_sb[:, c, w, :], in0=k_ps[:], scalar1=1.0, scalar2=None,
+                        op0=ALU.mult, op1=ALU.max, accum_out=bank_max[:, c, w : w + 1],
+                    )
+                if waiting is not None:
+                    quantise(*waiting)
+                    waiting = None
+                if round_ < len(later):
+                    blocks, codes, scales = later[round_]
+                    waiting = (transpose_group(blocks, False), codes, scales)
+                else:
+                    wo_grouped.append(transpose_group(last[round_ - len(later)][0], False))
+                if round_ == gate_round:
+                    gate_stage()
+                if round_ == rounds - 3:
+                    row_maxima(first_steps)
+                if round_ == rounds - 2:
+                    spread_first = spread_maxima(first_steps)
+                if round_ == rounds - 1:
+                    negated_maximum(spread_first, first_steps)
+
+            row_maxima(last_steps)
+            spread_last = spread_maxima(last_steps)
+            quantise(wo_grouped[0], last[0][1], last[0][2])
+            negated_maximum(spread_last, last_steps)
+
+        with tc.tile_pool(name="prod", bufs=3 * RUN) as prod, tc.tile_pool(name="small", bufs=2) as small, tc.tile_pool(
+            name="late", bufs=1
+        ) as late, tc.psum_pool(name="sums", bufs=1) as sums:
+            divisor = late.tile([P, CHUNKS, P, BLOCKS], F32, name="divisor")
+            h_codes = late.tile([P, CHUNKS, P], U32, name="h_codes", align_bytes=64)
+            h_scales = late.tile([P, CHUNKS, P], U8, name="h_scales", align_bytes=64)
+            out_sb = late.tile([P, L], F32, name="out_sb")
+            partial = late.tile([P, CHUNKS, CHUNK], F32, name="partial")
+            products = {}
+            numerator = {}
+
+            for c in range(CHUNKS):
+                for w in range(W):
+                    e = k_sb[:, c, w, :]
+                    nc.scalar.activation(out=e, in_=e, func=ACT.Exp, bias=neg_m[:, w : w + 1], scale=1.0)
+                    if w == 1:
+                        nc.gpsimd.tensor_tensor(out=partial[:, c, :], in0=k_sb[:, c, 0, :], in1=e, op=ALU.add)
+                    elif 1 < w < GPSIMD_STEPS:
+                        nc.gpsimd.tensor_tensor(out=partial[:, c, :], in0=partial[:, c, :], in1=e, op=ALU.add)
+
+            def add_transposed(bank, source, first, last):
+                for t in range(BLOCKS):
+                    nc.tensor.matmul(
+                        out=bank[:, t, :], lhsT=source[:, P * t : P * (t + 1)], rhs=ident[:], is_transpose=True,
+                        start=first and t == 0, stop=last and t == BLOCKS - 1,
+                    )
+
+            def multiply(c, steps):
+                for w in steps:
+                    v_ps = banks.tile([P, CHUNK], F32, name="v_ps", tag="bank")
+                    mx_pass(v_ps[:], z_codes, z_scales, step_cols(w), wv_codes, wv_scales, chunk_cols(c), True, True)
+                    ev = prod.tile([P, CHUNK], F32, name="ev")
+                    nc.vector.tensor_tensor(out=ev[:], in0=k_sb[:, c, w, :], in1=v_ps[:], op=ALU.mult)
+                    products[(c, w)] = ev
+
+            def sum_products(c, steps):
+                if c not in numerator:
+                    numerator[c] = sums.tile([P, BLOCKS, P], F32, name="numerator%d" % c)
+                for w in steps:
+                    add_transposed(numerator[c], products[(c, w)], w == 0, w == W - 1)
+
+            def reciprocal_divisor(c):
+                den_ps = banks.tile([P, BLOCKS, P], F32, name="den_ps", tag="bank")
+                add_transposed(den_ps, partial[:, c, :], True, False)
+                for w in range(GPSIMD_STEPS, W):
+                    add_transposed(den_ps, k_sb[:, c, w, :], False, w == W - 1)
+                nc.vector.scalar_tensor_tensor(
+                    out=divisor[:, c], in0=den_ps[:].rearrange("p t b -> p b t"), scalar=EPS, in1=gate[:, c],
+                    op0=ALU.add, op1=ALU.mult,
+                )
+                nc.scalar.activation(out=divisor[:, c], in_=divisor[:, c], func=ACT.Abs_reciprocal_sqrt)
+                nc.scalar.activation(out=divisor[:, c], in_=divisor[:, c], func=ACT.Square)
+
+            def hidden(c):
+                h = small.tile([P, P, BLOCKS], BF16, name="h", align_bytes=64)
+                nc.vector.tensor_tensor(out=h[:], in0=numerator[c][:].rearrange("p t b -> p b t"), in1=divisor[:, c], op=ALU.mult)
+                nc.vector.quantize_mx(out=h_codes[:, c, :].bitcast(FP8X4), scales=h_scales[:, c, :],
+                                      in_=h[:].rearrange("p b t -> p (b t)"))
+
+            runs = [(c, range(first, first + RUN)) for c in range(CHUNKS) for first in range(0, W, RUN)]
+            for i, (c, steps) in enumerate(runs):
+                multiply(c, steps)
+                if i + 1 < CHUNKS:
+                    quantise(wo_grouped[i + 1], last[i + 1][1], last[i + 1][2])
+                if i >= 1:
+                    sum_products(*runs[i - 1])
+                if steps[0] == 0 and c >= 1:
+                    reciprocal_divisor(c - 1)
+                if i > len(runs) - CHUNKS:
+                    hidden(i - len(runs) + CHUNKS - 1)
+            reciprocal_divisor(CHUNKS - 1)
+            sum_products(*runs[-1])
+            hidden(CHUNKS - 1)
+
+            out_ps = banks.tile([P, L], F32, name="out_ps", tag="bank")
+            for c in range(CHUNKS):
+                nc.tensor.matmul_mx(
+                    out=out_ps[:], lhsT=h_codes[:, c, :].bitcast(FP8X4), lhsT_scale=h_scales[:, c, :],
+                    rhs=wo_codes[:, chunk_cols(c)].bitcast(FP8X4), rhs_scale=wo_scales[:, chunk_cols(c)],
+                    start=c == 0, stop=c == CHUNKS - 1,
+                )
+            nc.scalar.copy(out=out_sb[:], in_=out_ps[:])
+            nc.sync.dma_start(out=out, in_=out_sb[:])

@@ -22,9 +22,10 @@ CHUNKS = A // CHUNK
 BLOCKS = CHUNK // P
 WORDS = L // 2
 GROUP = 4
+PAIR = 2
 ROUND = 2
 RUN = 4
-GPSIMD_STEPS = 6
+GPSIMD_STEPS = (6, 6, 6, 2)
 
 FLOPS = 2 * P * L * A * (1 + 2 * W) + 2 * P * A * L
 
@@ -56,6 +57,7 @@ def tile_aftblock_pa_kernel(tc, z_current, z_window, Wq, Wk, Wv, Wo, out):
         row_max = keep.tile([P, W], F32, name="row_max")
         neg_m = keep.tile([P, W], F32, name="neg_m")
         gate = keep.tile([P, CHUNKS, P, BLOCKS], F32, name="gate")
+        partial = keep.tile([P, CHUNKS, CHUNK], F32, name="partial")
 
         def mx_pass(acc, lhs_codes, lhs_scales, lhs_cols, rhs_codes, rhs_scales, rhs_cols, start, stop):
             nc.tensor.matmul_mx(
@@ -74,6 +76,14 @@ def tile_aftblock_pa_kernel(tc, z_current, z_window, Wq, Wk, Wv, Wo, out):
         def chunk_cols(c):
             return slice(c * CHUNK, (c + 1) * CHUNK)
 
+        def exponential(c, w):
+            e = k_sb[:, c, w, :]
+            nc.scalar.activation(out=e, in_=e, func=ACT.Exp, bias=neg_m[:, w : w + 1], scale=1.0)
+            if w == 1:
+                nc.gpsimd.tensor_tensor(out=partial[:, c, :], in0=k_sb[:, c, 0, :], in1=e, op=ALU.add)
+            elif 1 < w < GPSIMD_STEPS[c]:
+                nc.gpsimd.tensor_tensor(out=partial[:, c, :], in0=partial[:, c, :], in1=e, op=ALU.add)
+
         with tc.tile_pool(name="raw", bufs=1) as raw, tc.psum_pool(name="flip", bufs=4) as flip:
             z_raw = raw.tile([P, W + 1, L], BF16, name="z_raw")
             wk_raw = raw.tile([P, A // P, L], BF16, name="wk_raw")
@@ -81,22 +91,26 @@ def tile_aftblock_pa_kernel(tc, z_current, z_window, Wq, Wk, Wv, Wo, out):
             wq_raw = raw.tile([P, A // P, L], BF16, name="wq_raw")
             wo_raw = raw.tile([P, L // P, A], BF16, name="wo_raw")
 
-            def load_steps(first):
-                steps = slice(first, first + GROUP)
+            def load_steps(first, count):
+                steps = slice(first, first + count)
                 nc.sync.dma_start(out=z_raw[:, steps, :], in_=z_window[steps].rearrange("w b l -> b w l"))
 
-            def load_features(tile_, weight, c):
+            def load_features(tile_, weight, c, first=0, count=BLOCKS):
                 rows = weight.rearrange("(c r t) l -> r c t l", c=CHUNKS, t=BLOCKS)
-                nc.sync.dma_start(out=tile_[:, BLOCKS * c : BLOCKS * (c + 1), :], in_=rows[:, c])
+                start = BLOCKS * c + first
+                nc.sync.dma_start(out=tile_[:, start : start + count, :], in_=rows[:, c, first : first + count])
 
             def load_wo(g):
                 nc.sync.dma_start(out=wo_raw[:, :, chunk_cols(g)], in_=Wo.rearrange("(i p) a -> p i a", p=P)[:, :, chunk_cols(g)])
 
-            load_steps(0)
-            load_features(wk_raw, Wk, 0)
+            load_steps(0, PAIR)
+            load_features(wk_raw, Wk, 0, 0, PAIR)
+            load_features(wk_raw, Wk, 0, PAIR, PAIR)
+            load_steps(PAIR, PAIR)
+            load_steps(GROUP, GROUP)
+            load_features(wk_raw, Wk, 1)
             nc.sync.dma_start(out=z_raw[:, W, :], in_=z_current)
-            load_steps(GROUP)
-            for c in range(1, CHUNKS):
+            for c in range(2, CHUNKS):
                 load_features(wk_raw, Wk, c)
             for c in range(CHUNKS):
                 load_features(wq_raw, Wq, c)
@@ -105,18 +119,18 @@ def tile_aftblock_pa_kernel(tc, z_current, z_window, Wq, Wk, Wv, Wo, out):
             for g in range(CHUNKS):
                 load_wo(g)
 
-            def transpose_group(blocks, share_with_vector):
+            def transpose_group(blocks, on_vector=False):
                 grouped = stage.tile([P, len(blocks) * P * BLOCKS], BF16, name="grouped", align_bytes=64)
                 words = grouped[:].bitcast(F32).rearrange("p (k r u) -> p k r u", r=P, u=2)
-                for first in range(0, len(blocks), 2):
-                    pair = blocks[first : first + 2]
-                    flipped = flip.tile([P, 2, 2, P], F32, name="flipped")
+                for first in range(0, len(blocks), PAIR):
+                    pair = blocks[first : first + PAIR]
+                    flipped = flip.tile([P, PAIR, 2, P], F32, name="flipped")
                     for k, block in enumerate(pair):
                         for u in range(2):
                             nc.tensor.transpose(flipped[:, k, u, :], block[:, u : WORDS : 2], ident[:])
                     source = flipped[:, 0 : len(pair)].rearrange("p k u r -> p k r u")
                     target = words[:, first : first + len(pair)]
-                    if share_with_vector and first > 0:
+                    if on_vector:
                         nc.vector.tensor_copy(out=target, in_=source)
                     else:
                         nc.scalar.copy(out=target, in_=source)
@@ -125,9 +139,12 @@ def tile_aftblock_pa_kernel(tc, z_current, z_window, Wq, Wk, Wv, Wo, out):
             def quantise(grouped, codes, scales):
                 nc.vector.quantize_mx(out=codes.bitcast(FP8X4), scales=scales, in_=grouped[:])
 
+            def piece(blocks, codes, scales, first, count):
+                cols = slice(P * first, P * (first + count))
+                return blocks[first : first + count], codes[:, cols], scales[:, cols]
+
             def group_of(blocks, codes, scales, i):
-                cols = slice(GROUP * P * i, GROUP * P * (i + 1))
-                return blocks[GROUP * i : GROUP * (i + 1)], codes[:, cols], scales[:, cols]
+                return piece(blocks, codes, scales, GROUP * i, GROUP)
 
             z_blocks = [z_raw[:, s, :].bitcast(F32) for s in range(W + 1)]
             wk_blocks = [wk_raw[:, j, :].bitcast(F32) for j in range(A // P)]
@@ -139,16 +156,24 @@ def tile_aftblock_pa_kernel(tc, z_current, z_window, Wq, Wk, Wv, Wo, out):
                 for i in range(L // P)
             ]
 
-            for blocks, codes, scales in (group_of(z_blocks, z_codes, z_scales, 0), group_of(wk_blocks, wk_codes, wk_scales, 0)):
-                quantise(transpose_group(blocks, True), codes, scales)
-            waiting = (transpose_group(z_blocks[W:], False), z_codes[:, W * P :], z_scales[:, W * P :])
+            head = [
+                piece(z_blocks, z_codes, z_scales, 0, PAIR),
+                piece(wk_blocks, wk_codes, wk_scales, 0, PAIR),
+                piece(wk_blocks, wk_codes, wk_scales, PAIR, PAIR),
+                piece(z_blocks, z_codes, z_scales, PAIR, PAIR),
+            ]
+            waiting = [(transpose_group(blocks, i == 1), codes, scales) for i, (blocks, codes, scales) in enumerate(head)]
+            for ready in waiting[:-1]:
+                quantise(*ready)
+            waiting = waiting[-1:]
 
             later = (
-                [group_of(z_blocks, z_codes, z_scales, 1)]
-                + [group_of(wk_blocks, wk_codes, wk_scales, c) for c in range(1, CHUNKS)]
-                + [group_of(wq_blocks, wq_codes, wq_scales, c) for c in range(CHUNKS)]
-                + [group_of(wv_blocks, wv_codes, wv_scales, c) for c in range(CHUNKS)]
+                [[group_of(z_blocks, z_codes, z_scales, 1)]]
+                + [[group_of(wk_blocks, wk_codes, wk_scales, c)] for c in range(1, CHUNKS)]
+                + [[group_of(wq_blocks, wq_codes, wq_scales, c)] for c in range(CHUNKS)]
+                + [[group_of(wv_blocks, wv_codes, wv_scales, c)] for c in range(CHUNKS)]
             )
+            later[1].append(piece(z_blocks, z_codes, z_scales, W, 1))
             last = [group_of(wo_blocks, wo_codes, wo_scales, g) for g in range(CHUNKS)]
             gate_round = len(later) - CHUNKS + 2
 
@@ -179,38 +204,42 @@ def tile_aftblock_pa_kernel(tc, z_current, z_window, Wq, Wk, Wv, Wo, out):
 
             first_steps = 0
             last_steps = BLOCKS
+            half = CHUNKS // 2
+            k_order = [(c, w) for c in range(half) for w in range(W)]
+            for first in (first_steps, last_steps):
+                k_order += [(c, w) for c in range(half, CHUNKS) for w in range(first, first + BLOCKS)]
             wo_grouped = []
             rounds = CHUNKS * W // ROUND
+            first_known = rounds - half * BLOCKS // ROUND
+            early = 0
             for round_ in range(rounds):
-                for bank in range(ROUND * round_, ROUND * (round_ + 1)):
-                    c, w = divmod(bank, W)
+                for c, w in k_order[ROUND * round_ : ROUND * (round_ + 1)]:
                     k_ps = banks.tile([P, CHUNK], F32, name="k_ps", tag="bank")
                     mx_pass(k_ps[:], z_codes, z_scales, step_cols(w), wk_codes, wk_scales, chunk_cols(c), True, True)
                     nc.vector.tensor_scalar(
                         out=k_sb[:, c, w, :], in0=k_ps[:], scalar1=1.0, scalar2=None,
                         op0=ALU.mult, op1=ALU.max, accum_out=bank_max[:, c, w : w + 1],
                     )
-                if waiting is not None:
-                    quantise(*waiting)
-                    waiting = None
+                for ready in waiting:
+                    quantise(*ready)
+                waiting = []
                 if round_ < len(later):
-                    blocks, codes, scales = later[round_]
-                    waiting = (transpose_group(blocks, False), codes, scales)
+                    waiting = [(transpose_group(blocks), codes, scales) for blocks, codes, scales in later[round_]]
                 else:
-                    wo_grouped.append(transpose_group(last[round_ - len(later)][0], False))
+                    wo_grouped.append(transpose_group(last[round_ - len(later)][0]))
                 if round_ == gate_round:
                     gate_stage()
-                if round_ == rounds - 3:
+                if round_ == first_known - 1:
                     row_maxima(first_steps)
-                if round_ == rounds - 2:
+                if round_ == first_known:
                     spread_first = spread_maxima(first_steps)
-                if round_ == rounds - 1:
+                if round_ == first_known + 1:
                     negated_maximum(spread_first, first_steps)
+                if round_ > first_known + 1:
+                    exponential(0, early)
+                    early += 1
 
             row_maxima(last_steps)
-            spread_last = spread_maxima(last_steps)
-            quantise(wo_grouped[0], last[0][1], last[0][2])
-            negated_maximum(spread_last, last_steps)
 
         with tc.tile_pool(name="prod", bufs=3 * RUN) as prod, tc.tile_pool(name="small", bufs=2) as small, tc.tile_pool(
             name="late", bufs=1
@@ -219,18 +248,11 @@ def tile_aftblock_pa_kernel(tc, z_current, z_window, Wq, Wk, Wv, Wo, out):
             h_codes = late.tile([P, CHUNKS, P], U32, name="h_codes", align_bytes=64)
             h_scales = late.tile([P, CHUNKS, P], U8, name="h_scales", align_bytes=64)
             out_sb = late.tile([P, L], F32, name="out_sb")
-            partial = late.tile([P, CHUNKS, CHUNK], F32, name="partial")
             products = {}
             numerator = {}
 
-            for c in range(CHUNKS):
-                for w in range(W):
-                    e = k_sb[:, c, w, :]
-                    nc.scalar.activation(out=e, in_=e, func=ACT.Exp, bias=neg_m[:, w : w + 1], scale=1.0)
-                    if w == 1:
-                        nc.gpsimd.tensor_tensor(out=partial[:, c, :], in0=k_sb[:, c, 0, :], in1=e, op=ALU.add)
-                    elif 1 < w < GPSIMD_STEPS:
-                        nc.gpsimd.tensor_tensor(out=partial[:, c, :], in0=partial[:, c, :], in1=e, op=ALU.add)
+            for w in range(early, BLOCKS):
+                exponential(0, w)
 
             def add_transposed(bank, source, first, last):
                 for t in range(BLOCKS):
@@ -239,13 +261,12 @@ def tile_aftblock_pa_kernel(tc, z_current, z_window, Wq, Wk, Wv, Wo, out):
                         start=first and t == 0, stop=last and t == BLOCKS - 1,
                     )
 
-            def multiply(c, steps):
-                for w in steps:
-                    v_ps = banks.tile([P, CHUNK], F32, name="v_ps", tag="bank")
-                    mx_pass(v_ps[:], z_codes, z_scales, step_cols(w), wv_codes, wv_scales, chunk_cols(c), True, True)
-                    ev = prod.tile([P, CHUNK], F32, name="ev")
-                    nc.vector.tensor_tensor(out=ev[:], in0=k_sb[:, c, w, :], in1=v_ps[:], op=ALU.mult)
-                    products[(c, w)] = ev
+            def multiply(c, w):
+                v_ps = banks.tile([P, CHUNK], F32, name="v_ps", tag="bank")
+                mx_pass(v_ps[:], z_codes, z_scales, step_cols(w), wv_codes, wv_scales, chunk_cols(c), True, True)
+                ev = prod.tile([P, CHUNK], F32, name="ev")
+                nc.vector.tensor_tensor(out=ev[:], in0=k_sb[:, c, w, :], in1=v_ps[:], op=ALU.mult)
+                products[(c, w)] = ev
 
             def sum_products(c, steps):
                 if c not in numerator:
@@ -253,11 +274,14 @@ def tile_aftblock_pa_kernel(tc, z_current, z_window, Wq, Wk, Wv, Wo, out):
                 for w in steps:
                     add_transposed(numerator[c], products[(c, w)], w == 0, w == W - 1)
 
-            def reciprocal_divisor(c):
+            def denominator(c):
                 den_ps = banks.tile([P, BLOCKS, P], F32, name="den_ps", tag="bank")
                 add_transposed(den_ps, partial[:, c, :], True, False)
-                for w in range(GPSIMD_STEPS, W):
+                for w in range(GPSIMD_STEPS[c], W):
                     add_transposed(den_ps, k_sb[:, c, w, :], False, w == W - 1)
+                return den_ps
+
+            def reciprocal_divisor(c, den_ps):
                 nc.vector.scalar_tensor_tensor(
                     out=divisor[:, c], in0=den_ps[:].rearrange("p t b -> p b t"), scalar=EPS, in1=gate[:, c],
                     op0=ALU.add, op1=ALU.mult,
@@ -272,17 +296,34 @@ def tile_aftblock_pa_kernel(tc, z_current, z_window, Wq, Wk, Wv, Wo, out):
                                       in_=h[:].rearrange("p b t -> p (b t)"))
 
             runs = [(c, range(first, first + RUN)) for c in range(CHUNKS) for first in range(0, W, RUN)]
+            last_run = len(runs) - 1
+            dens = []
+            done = 0
             for i, (c, steps) in enumerate(runs):
-                multiply(c, steps)
-                if i + 1 < CHUNKS:
-                    quantise(wo_grouped[i + 1], last[i + 1][1], last[i + 1][2])
+                for n, w in enumerate(steps):
+                    multiply(c, w)
+                    if n != RUN // 2 - 1:
+                        continue
+                    if i == 0:
+                        spread_last = spread_maxima(last_steps)
+                        negated_maximum(spread_last, last_steps)
+                        for cc in range(CHUNKS):
+                            for ww in range(BLOCKS if cc == 0 else 0, W):
+                                exponential(cc, ww)
+                    for den in dens:
+                        reciprocal_divisor(done, den)
+                        done += 1
+                    dens = []
+                if i < CHUNKS:
+                    quantise(wo_grouped[i], last[i][1], last[i][2])
                 if i >= 1:
                     sum_products(*runs[i - 1])
-                if steps[0] == 0 and c >= 1:
-                    reciprocal_divisor(c - 1)
-                if i > len(runs) - CHUNKS:
-                    hidden(i - len(runs) + CHUNKS - 1)
-            reciprocal_divisor(CHUNKS - 1)
+                if i in (2, 4, last_run - 1):
+                    dens.append(denominator(c - 1))
+                if i == last_run - 1:
+                    dens.append(denominator(c))
+                if i >= last_run - 2:
+                    hidden(i - last_run + 2)
             sum_products(*runs[-1])
             hidden(CHUNKS - 1)
 

@@ -23,9 +23,10 @@ BLOCKS = CHUNK // P
 WORDS = L // 2
 GROUP = 4
 PAIR = 2
+GATE_LAG = 3
 ROUND = 2
 RUN = 4
-GPSIMD_STEPS = (6, 6, 6, 2)
+GPSIMD_STEPS = (6, 6, 5, 3)
 
 FLOPS = 2 * P * L * A * (1 + 2 * W) + 2 * P * A * L
 
@@ -119,7 +120,7 @@ def tile_aftblock_pa_kernel(tc, z_current, z_window, Wq, Wk, Wv, Wo, out):
             for g in range(CHUNKS):
                 load_wo(g)
 
-            def transpose_group(blocks, on_vector=False):
+            def transpose_group(blocks, on_vector=()):
                 grouped = stage.tile([P, len(blocks) * P * BLOCKS], BF16, name="grouped", align_bytes=64)
                 words = grouped[:].bitcast(F32).rearrange("p (k r u) -> p k r u", r=P, u=2)
                 for first in range(0, len(blocks), PAIR):
@@ -130,7 +131,7 @@ def tile_aftblock_pa_kernel(tc, z_current, z_window, Wq, Wk, Wv, Wo, out):
                             nc.tensor.transpose(flipped[:, k, u, :], block[:, u : WORDS : 2], ident[:])
                     source = flipped[:, 0 : len(pair)].rearrange("p k u r -> p k r u")
                     target = words[:, first : first + len(pair)]
-                    if on_vector:
+                    if first in on_vector:
                         nc.vector.tensor_copy(out=target, in_=source)
                     else:
                         nc.scalar.copy(out=target, in_=source)
@@ -162,7 +163,7 @@ def tile_aftblock_pa_kernel(tc, z_current, z_window, Wq, Wk, Wv, Wo, out):
                 piece(wk_blocks, wk_codes, wk_scales, PAIR, PAIR),
                 piece(z_blocks, z_codes, z_scales, PAIR, PAIR),
             ]
-            waiting = [(transpose_group(blocks, i == 1), codes, scales) for i, (blocks, codes, scales) in enumerate(head)]
+            waiting = [(transpose_group(blocks, (0,) if i == 1 else ()), codes, scales) for i, (blocks, codes, scales) in enumerate(head)]
             for ready in waiting[:-1]:
                 quantise(*ready)
             waiting = waiting[-1:]
@@ -174,17 +175,16 @@ def tile_aftblock_pa_kernel(tc, z_current, z_window, Wq, Wk, Wv, Wo, out):
                 + [[group_of(wv_blocks, wv_codes, wv_scales, c)] for c in range(CHUNKS)]
             )
             later[1].append(piece(z_blocks, z_codes, z_scales, W, 1))
-            last = [group_of(wo_blocks, wo_codes, wo_scales, g) for g in range(CHUNKS)]
-            gate_round = len(later) - CHUNKS + 2
+            wo_rounds = len(later)
+            later += [[group_of(wo_blocks, wo_codes, wo_scales, g)] for g in range(CHUNKS)]
 
-            def gate_stage():
-                for c in range(CHUNKS):
-                    q_ps = flip.tile([P, BLOCKS, P], F32, name="q_ps", tag="flipped")
-                    for t in range(BLOCKS):
-                        mx_pass(q_ps[:, t, :], wq_codes, wq_scales, step_cols(BLOCKS * c + t),
-                                z_codes, z_scales, step_cols(W), True, True)
-                    nc.scalar.activation(out=gate[:, c], in_=q_ps[:].rearrange("p t b -> p b t"), func=ACT.Exp, scale=-1.0)
-                flat = gate[:].rearrange("p c b t -> p (c b t)")
+            def gate_chunk(c):
+                q_ps = flip.tile([P, BLOCKS, P], F32, name="q_ps", tag="flipped")
+                for t in range(BLOCKS):
+                    mx_pass(q_ps[:, t, :], wq_codes, wq_scales, step_cols(BLOCKS * c + t),
+                            z_codes, z_scales, step_cols(W), True, True)
+                nc.scalar.activation(out=gate[:, c], in_=q_ps[:].rearrange("p t b -> p b t"), func=ACT.Exp, scale=-1.0)
+                flat = gate[:, c].rearrange("p b t -> p (b t)")
                 nc.gpsimd.tensor_scalar(out=flat, in0=flat, scalar1=1.0, scalar2=1.0, op0=ALU.add, op1=ALU.mult)
 
             def row_maxima(first):
@@ -204,55 +204,53 @@ def tile_aftblock_pa_kernel(tc, z_current, z_window, Wq, Wk, Wv, Wo, out):
 
             first_steps = 0
             last_steps = BLOCKS
-            half = CHUNKS // 2
-            k_order = [(c, w) for c in range(half) for w in range(W)]
+            k_order = [(0, w) for w in range(W)]
             for first in (first_steps, last_steps):
-                k_order += [(c, w) for c in range(half, CHUNKS) for w in range(first, first + BLOCKS)]
-            wo_grouped = []
-            rounds = CHUNKS * W // ROUND
-            first_known = rounds - half * BLOCKS // ROUND
-            early = 0
+                k_order += [(c, w) for c in range(1, CHUNKS) for w in range(first, first + BLOCKS)]
+            rounds = len(later)
+            first_known = rounds - (CHUNKS - 1) * BLOCKS // ROUND
+            early = [(c, w) for c in range(2) for w in range(BLOCKS)]
+            wo_waiting = []
             for round_ in range(rounds):
-                for c, w in k_order[ROUND * round_ : ROUND * (round_ + 1)]:
+                for n, (c, w) in enumerate(k_order[ROUND * round_ : ROUND * (round_ + 1)]):
                     k_ps = banks.tile([P, CHUNK], F32, name="k_ps", tag="bank")
                     mx_pass(k_ps[:], z_codes, z_scales, step_cols(w), wk_codes, wk_scales, chunk_cols(c), True, True)
                     nc.vector.tensor_scalar(
                         out=k_sb[:, c, w, :], in0=k_ps[:], scalar1=1.0, scalar2=None,
                         op0=ALU.mult, op1=ALU.max, accum_out=bank_max[:, c, w : w + 1],
                     )
-                for ready in waiting:
-                    quantise(*ready)
-                waiting = []
-                if round_ < len(later):
-                    waiting = [(transpose_group(blocks), codes, scales) for blocks, codes, scales in later[round_]]
-                else:
-                    wo_grouped.append(transpose_group(last[round_ - len(later)][0]))
-                if round_ == gate_round:
-                    gate_stage()
+                    for ready in waiting:
+                        quantise(*ready)
+                    waiting = []
+                if 0 <= round_ - CHUNKS - GATE_LAG < CHUNKS:
+                    gate_chunk(round_ - CHUNKS - GATE_LAG)
                 if round_ == first_known - 1:
                     row_maxima(first_steps)
-                if round_ == first_known:
-                    spread_first = spread_maxima(first_steps)
                 if round_ == first_known + 1:
                     negated_maximum(spread_first, first_steps)
-                if round_ > first_known + 1:
-                    exponential(0, early)
-                    early += 1
+                on_vector = (PAIR,) if round_ >= wo_rounds else ()
+                flipped_groups = [(transpose_group(blocks, on_vector), codes, scales) for blocks, codes, scales in later[round_]]
+                if round_ < wo_rounds:
+                    waiting = flipped_groups
+                else:
+                    wo_waiting += flipped_groups
+                if round_ == first_known:
+                    spread_first = spread_maxima(first_steps)
+                if round_ >= wo_rounds:
+                    for c, w in early[2 * (round_ - wo_rounds) : 2 * (round_ - wo_rounds + 1)]:
+                        exponential(c, w)
 
             row_maxima(last_steps)
 
         with tc.tile_pool(name="prod", bufs=3 * RUN) as prod, tc.tile_pool(name="small", bufs=2) as small, tc.tile_pool(
             name="late", bufs=1
-        ) as late, tc.psum_pool(name="sums", bufs=1) as sums:
+        ) as late, tc.psum_pool(name="sums", bufs=CHUNKS - 1) as sums, tc.psum_pool(name="dens", bufs=1) as dens:
             divisor = late.tile([P, CHUNKS, P, BLOCKS], F32, name="divisor")
             h_codes = late.tile([P, CHUNKS, P], U32, name="h_codes", align_bytes=64)
             h_scales = late.tile([P, CHUNKS, P], U8, name="h_scales", align_bytes=64)
             out_sb = late.tile([P, L], F32, name="out_sb")
             products = {}
             numerator = {}
-
-            for w in range(early, BLOCKS):
-                exponential(0, w)
 
             def add_transposed(bank, source, first, last):
                 for t in range(BLOCKS):
@@ -261,21 +259,24 @@ def tile_aftblock_pa_kernel(tc, z_current, z_window, Wq, Wk, Wv, Wo, out):
                         start=first and t == 0, stop=last and t == BLOCKS - 1,
                     )
 
-            def multiply(c, w):
+            def v_pass(c, w):
                 v_ps = banks.tile([P, CHUNK], F32, name="v_ps", tag="bank")
                 mx_pass(v_ps[:], z_codes, z_scales, step_cols(w), wv_codes, wv_scales, chunk_cols(c), True, True)
+                return v_ps
+
+            def multiply(c, w, v_ps):
                 ev = prod.tile([P, CHUNK], F32, name="ev")
                 nc.vector.tensor_tensor(out=ev[:], in0=k_sb[:, c, w, :], in1=v_ps[:], op=ALU.mult)
                 products[(c, w)] = ev
 
             def sum_products(c, steps):
                 if c not in numerator:
-                    numerator[c] = sums.tile([P, BLOCKS, P], F32, name="numerator%d" % c)
+                    numerator[c] = sums.tile([P, BLOCKS, P], F32, name="sum_ps")
                 for w in steps:
                     add_transposed(numerator[c], products[(c, w)], w == 0, w == W - 1)
 
             def denominator(c):
-                den_ps = banks.tile([P, BLOCKS, P], F32, name="den_ps", tag="bank")
+                den_ps = dens.tile([P, BLOCKS, P], F32, name="den_ps")
                 add_transposed(den_ps, partial[:, c, :], True, False)
                 for w in range(GPSIMD_STEPS[c], W):
                     add_transposed(den_ps, k_sb[:, c, w, :], False, w == W - 1)
@@ -297,33 +298,36 @@ def tile_aftblock_pa_kernel(tc, z_current, z_window, Wq, Wk, Wv, Wo, out):
 
             runs = [(c, range(first, first + RUN)) for c in range(CHUNKS) for first in range(0, W, RUN)]
             last_run = len(runs) - 1
-            dens = []
-            done = 0
+            den_runs = {2: 0, 4: 1, 5: 2, 6: 3}
+            hidden_after = {6: 0, 7: 2}
+            hidden_in = {7: 1}
             for i, (c, steps) in enumerate(runs):
                 for n, w in enumerate(steps):
-                    multiply(c, w)
-                    if n != RUN // 2 - 1:
-                        continue
-                    if i == 0:
+                    if i == 0 and n == 0:
+                        ahead = [v_pass(c, w), v_pass(c, w + 1)]
+                        multiply(c, w, ahead[0])
                         spread_last = spread_maxima(last_steps)
                         negated_maximum(spread_last, last_steps)
-                        for cc in range(CHUNKS):
-                            for ww in range(BLOCKS if cc == 0 else 0, W):
-                                exponential(cc, ww)
-                    for den in dens:
-                        reciprocal_divisor(done, den)
-                        done += 1
-                    dens = []
-                if i < CHUNKS:
-                    quantise(wo_grouped[i], last[i][1], last[i][2])
+                        for late_c in range(CHUNKS):
+                            for late_w in range(W):
+                                if (late_c, late_w) not in early:
+                                    exponential(late_c, late_w)
+                    elif i == 0 and n == 1:
+                        multiply(c, w, ahead[1])
+                    else:
+                        multiply(c, w, v_pass(c, w))
+                    if n == 0 and i - 1 in den_runs:
+                        reciprocal_divisor(den_runs[i - 1], den_ps)
+                    if n == 1 and i in hidden_in:
+                        hidden(hidden_in[i])
                 if i >= 1:
                     sum_products(*runs[i - 1])
-                if i in (2, 4, last_run - 1):
-                    dens.append(denominator(c - 1))
-                if i == last_run - 1:
-                    dens.append(denominator(c))
-                if i >= last_run - 2:
-                    hidden(i - last_run + 2)
+                if i in den_runs:
+                    den_ps = denominator(den_runs[i])
+                if last_run - CHUNKS <= i < last_run:
+                    quantise(*wo_waiting[i - last_run + CHUNKS])
+                if i in hidden_after:
+                    hidden(hidden_after[i])
             sum_products(*runs[-1])
             hidden(CHUNKS - 1)
 

@@ -26,7 +26,7 @@ PAIR = 2
 GATE_LAG = 3
 ROUND = 2
 RUN = 4
-GPSIMD_STEPS = (6, 6, 5, 3)
+GPSIMD_STEPS = (7, 7, 6, 4)
 
 FLOPS = 2 * P * L * A * (1 + 2 * W) + 2 * P * A * L
 
@@ -85,6 +85,11 @@ def tile_aftblock_pa_kernel(tc, z_current, z_window, Wq, Wk, Wv, Wo, out):
             elif 1 < w < GPSIMD_STEPS[c]:
                 nc.gpsimd.tensor_tensor(out=partial[:, c, :], in0=partial[:, c, :], in1=e, op=ALU.add)
 
+        def v_pass(c, w):
+            v_ps = banks.tile([P, CHUNK], F32, name="v_ps", tag="bank")
+            mx_pass(v_ps[:], z_codes, z_scales, step_cols(w), wv_codes, wv_scales, chunk_cols(c), True, True)
+            return v_ps
+
         with tc.tile_pool(name="raw", bufs=1) as raw, tc.psum_pool(name="flip", bufs=4) as flip:
             z_raw = raw.tile([P, W + 1, L], BF16, name="z_raw")
             wk_raw = raw.tile([P, A // P, L], BF16, name="wk_raw")
@@ -104,15 +109,25 @@ def tile_aftblock_pa_kernel(tc, z_current, z_window, Wq, Wk, Wv, Wo, out):
             def load_wo(g):
                 nc.sync.dma_start(out=wo_raw[:, :, chunk_cols(g)], in_=Wo.rearrange("(i p) a -> p i a", p=P)[:, :, chunk_cols(g)])
 
+            zeros = keep.tile([P, CHUNK], BF16, name="zeros")
+            nc.vector.memset(zeros[:], 0.0)
+
+            def warm_up(count):
+                for n in range(count):
+                    dummy = banks.tile([P, CHUNK], F32, name="dummy", tag="bank")
+                    nc.tensor.matmul(out=dummy[:], lhsT=zeros[:, :P], rhs=zeros[:], start=True, stop=True)
+
+            warm_up(3)
+
             load_steps(0, PAIR)
             load_features(wk_raw, Wk, 0, 0, PAIR)
-            load_features(wk_raw, Wk, 0, PAIR, PAIR)
+            for first in range(PAIR, BLOCKS):
+                load_features(wk_raw, Wk, 0, first, 1)
             load_steps(PAIR, PAIR)
-            load_steps(GROUP, GROUP)
-            load_features(wk_raw, Wk, 1)
-            nc.sync.dma_start(out=z_raw[:, W, :], in_=z_current)
-            for c in range(2, CHUNKS):
+            for c in range(1, CHUNKS):
                 load_features(wk_raw, Wk, c)
+            load_steps(GROUP, GROUP)
+            nc.sync.dma_start(out=z_raw[:, W, :], in_=z_current)
             for c in range(CHUNKS):
                 load_features(wq_raw, Wq, c)
             for c in range(CHUNKS):
@@ -160,21 +175,23 @@ def tile_aftblock_pa_kernel(tc, z_current, z_window, Wq, Wk, Wv, Wo, out):
             head = [
                 piece(z_blocks, z_codes, z_scales, 0, PAIR),
                 piece(wk_blocks, wk_codes, wk_scales, 0, PAIR),
-                piece(wk_blocks, wk_codes, wk_scales, PAIR, PAIR),
+                piece(wk_blocks, wk_codes, wk_scales, PAIR, 1),
+                piece(wk_blocks, wk_codes, wk_scales, PAIR + 1, 1),
                 piece(z_blocks, z_codes, z_scales, PAIR, PAIR),
             ]
-            waiting = [(transpose_group(blocks, (0,) if i == 1 else ()), codes, scales) for i, (blocks, codes, scales) in enumerate(head)]
+            waiting = []
+            for i, (blocks, codes, scales) in enumerate(head):
+                waiting.append((transpose_group(blocks, (0,) if i % 2 == 1 else ()), codes, scales))
             for ready in waiting[:-1]:
                 quantise(*ready)
             waiting = waiting[-1:]
 
             later = (
-                [[group_of(z_blocks, z_codes, z_scales, 1)]]
-                + [[group_of(wk_blocks, wk_codes, wk_scales, c)] for c in range(1, CHUNKS)]
+                [[group_of(wk_blocks, wk_codes, wk_scales, c)] for c in range(1, CHUNKS)]
+                + [[group_of(z_blocks, z_codes, z_scales, 1), piece(z_blocks, z_codes, z_scales, W, 1)]]
                 + [[group_of(wq_blocks, wq_codes, wq_scales, c)] for c in range(CHUNKS)]
                 + [[group_of(wv_blocks, wv_codes, wv_scales, c)] for c in range(CHUNKS)]
             )
-            later[1].append(piece(z_blocks, z_codes, z_scales, W, 1))
             wo_rounds = len(later)
             later += [[group_of(wo_blocks, wo_codes, wo_scales, g)] for g in range(CHUNKS)]
 
@@ -194,7 +211,7 @@ def tile_aftblock_pa_kernel(tc, z_current, z_window, Wq, Wk, Wv, Wo, out):
                 )
 
             def spread_maxima(first):
-                spread = banks.tile([P, BLOCKS, P], F32, name="spread", tag="bank")
+                spread = flip.tile([P, BLOCKS, P], F32, name="spread", tag="flipped")
                 for i in range(BLOCKS):
                     nc.tensor.transpose(spread[:, i, :], row_max[:, first + i : first + i + 1].to_broadcast([P, P]), ident[:])
                 return spread
@@ -204,12 +221,12 @@ def tile_aftblock_pa_kernel(tc, z_current, z_window, Wq, Wk, Wv, Wo, out):
 
             first_steps = 0
             last_steps = BLOCKS
-            k_order = [(0, w) for w in range(W)]
-            for first in (first_steps, last_steps):
-                k_order += [(c, w) for c in range(1, CHUNKS) for w in range(first, first + BLOCKS)]
+            k_order = [(c, w) for first in (first_steps, last_steps) for c in range(CHUNKS) for w in range(first, first + BLOCKS)]
             rounds = len(later)
-            first_known = rounds - (CHUNKS - 1) * BLOCKS // ROUND
-            early = [(c, w) for c in range(2) for w in range(BLOCKS)]
+            first_known = rounds // 2
+            exps = [1 if round_ < wo_rounds else 2 for round_ in range(wo_rounds - 2, rounds)]
+            early = [(c, w) for c in range(CHUNKS) for w in range(BLOCKS)][: sum(exps)]
+            early_done = 0
             wo_waiting = []
             for round_ in range(rounds):
                 for n, (c, w) in enumerate(k_order[ROUND * round_ : ROUND * (round_ + 1)]):
@@ -236,11 +253,21 @@ def tile_aftblock_pa_kernel(tc, z_current, z_window, Wq, Wk, Wv, Wo, out):
                     wo_waiting += flipped_groups
                 if round_ == first_known:
                     spread_first = spread_maxima(first_steps)
-                if round_ >= wo_rounds:
-                    for c, w in early[2 * (round_ - wo_rounds) : 2 * (round_ - wo_rounds + 1)]:
+                if round_ >= wo_rounds - 2:
+                    count = exps[round_ - wo_rounds + 2]
+                    for c, w in early[early_done : early_done + count]:
                         exponential(c, w)
+                    early_done += count
 
             row_maxima(last_steps)
+            ahead = [v_pass(0, w) for w in range(2)]
+            spread_last = spread_maxima(last_steps)
+            quantise(*wo_waiting[0])
+            negated_maximum(spread_last, last_steps)
+            for c in range(CHUNKS):
+                for w in range(W):
+                    if (c, w) not in early:
+                        exponential(c, w)
 
         with tc.tile_pool(name="prod", bufs=3 * RUN) as prod, tc.tile_pool(name="small", bufs=2) as small, tc.tile_pool(
             name="late", bufs=1
@@ -258,11 +285,6 @@ def tile_aftblock_pa_kernel(tc, z_current, z_window, Wq, Wk, Wv, Wo, out):
                         out=bank[:, t, :], lhsT=source[:, P * t : P * (t + 1)], rhs=ident[:], is_transpose=True,
                         start=first and t == 0, stop=last and t == BLOCKS - 1,
                     )
-
-            def v_pass(c, w):
-                v_ps = banks.tile([P, CHUNK], F32, name="v_ps", tag="bank")
-                mx_pass(v_ps[:], z_codes, z_scales, step_cols(w), wv_codes, wv_scales, chunk_cols(c), True, True)
-                return v_ps
 
             def multiply(c, w, v_ps):
                 ev = prod.tile([P, CHUNK], F32, name="ev")
@@ -303,19 +325,7 @@ def tile_aftblock_pa_kernel(tc, z_current, z_window, Wq, Wk, Wv, Wo, out):
             hidden_in = {7: 1}
             for i, (c, steps) in enumerate(runs):
                 for n, w in enumerate(steps):
-                    if i == 0 and n == 0:
-                        ahead = [v_pass(c, w), v_pass(c, w + 1)]
-                        multiply(c, w, ahead[0])
-                        spread_last = spread_maxima(last_steps)
-                        negated_maximum(spread_last, last_steps)
-                        for late_c in range(CHUNKS):
-                            for late_w in range(W):
-                                if (late_c, late_w) not in early:
-                                    exponential(late_c, late_w)
-                    elif i == 0 and n == 1:
-                        multiply(c, w, ahead[1])
-                    else:
-                        multiply(c, w, v_pass(c, w))
+                    multiply(c, w, ahead.pop(0) if ahead else v_pass(c, w))
                     if n == 0 and i - 1 in den_runs:
                         reciprocal_divisor(den_runs[i - 1], den_ps)
                     if n == 1 and i in hidden_in:
@@ -324,19 +334,24 @@ def tile_aftblock_pa_kernel(tc, z_current, z_window, Wq, Wk, Wv, Wo, out):
                     sum_products(*runs[i - 1])
                 if i in den_runs:
                     den_ps = denominator(den_runs[i])
-                if last_run - CHUNKS <= i < last_run:
+                if last_run - CHUNKS < i < last_run:
                     quantise(*wo_waiting[i - last_run + CHUNKS])
                 if i in hidden_after:
                     hidden(hidden_after[i])
             sum_products(*runs[-1])
             hidden(CHUNKS - 1)
 
-            out_ps = banks.tile([P, L], F32, name="out_ps", tag="bank")
+            half_l = L // 2
+            out_ps = [banks.tile([P, half_l], F32, name="out_ps%d" % s, tag="bank") for s in range(2)]
             for c in range(CHUNKS):
-                nc.tensor.matmul_mx(
-                    out=out_ps[:], lhsT=h_codes[:, c, :].bitcast(FP8X4), lhsT_scale=h_scales[:, c, :],
-                    rhs=wo_codes[:, chunk_cols(c)].bitcast(FP8X4), rhs_scale=wo_scales[:, chunk_cols(c)],
-                    start=c == 0, stop=c == CHUNKS - 1,
-                )
-            nc.scalar.copy(out=out_sb[:], in_=out_ps[:])
-            nc.sync.dma_start(out=out, in_=out_sb[:])
+                for s in range(2):
+                    cols = slice(c * L + s * half_l, c * L + (s + 1) * half_l)
+                    nc.tensor.matmul_mx(
+                        out=out_ps[s][:], lhsT=h_codes[:, c, :].bitcast(FP8X4), lhsT_scale=h_scales[:, c, :],
+                        rhs=wo_codes[:, cols].bitcast(FP8X4), rhs_scale=wo_scales[:, cols],
+                        start=c == 0, stop=c == CHUNKS - 1,
+                    )
+            nc.scalar.copy(out=out_sb[:, :half_l], in_=out_ps[0][:])
+            nc.scalar.dma_start(out=out[:, :half_l], in_=out_sb[:, :half_l])
+            nc.vector.tensor_copy(out=out_sb[:, half_l:], in_=out_ps[1][:])
+            nc.sync.dma_start(out=out[:, half_l:], in_=out_sb[:, half_l:])

@@ -23,10 +23,11 @@ BLOCKS = CHUNK // P
 WORDS = L // 2
 GROUP = 4
 PAIR = 2
+EARLY_ROUND = 10
 GATE_LAG = 3
 ROUND = 2
 RUN = 4
-GPSIMD_STEPS = (7, 7, 6, 4)
+GPSIMD_STEPS = (6, 6, 5, 3)
 
 FLOPS = 2 * P * L * A * (1 + 2 * W) + 2 * P * A * L
 
@@ -117,7 +118,7 @@ def tile_aftblock_pa_kernel(tc, z_current, z_window, Wq, Wk, Wv, Wo, out):
                     dummy = banks.tile([P, CHUNK], F32, name="dummy", tag="bank")
                     nc.tensor.matmul(out=dummy[:], lhsT=zeros[:, :P], rhs=zeros[:], start=True, stop=True)
 
-            warm_up(3)
+            warm_up(2)
 
             load_steps(0, PAIR)
             load_features(wk_raw, Wk, 0, 0, PAIR)
@@ -181,7 +182,7 @@ def tile_aftblock_pa_kernel(tc, z_current, z_window, Wq, Wk, Wv, Wo, out):
             ]
             waiting = []
             for i, (blocks, codes, scales) in enumerate(head):
-                waiting.append((transpose_group(blocks, (0,) if i % 2 == 1 else ()), codes, scales))
+                waiting.append((transpose_group(blocks, (0,) if i == 1 else ()), codes, scales))
             for ready in waiting[:-1]:
                 quantise(*ready)
             waiting = waiting[-1:]
@@ -224,9 +225,7 @@ def tile_aftblock_pa_kernel(tc, z_current, z_window, Wq, Wk, Wv, Wo, out):
             k_order = [(c, w) for first in (first_steps, last_steps) for c in range(CHUNKS) for w in range(first, first + BLOCKS)]
             rounds = len(later)
             first_known = rounds // 2
-            exps = [1 if round_ < wo_rounds else 2 for round_ in range(wo_rounds - 2, rounds)]
-            early = [(c, w) for c in range(CHUNKS) for w in range(BLOCKS)][: sum(exps)]
-            early_done = 0
+            early = [(c, w) for c in range(CHUNKS) for w in range(BLOCKS)][: rounds - EARLY_ROUND]
             wo_waiting = []
             for round_ in range(rounds):
                 for n, (c, w) in enumerate(k_order[ROUND * round_ : ROUND * (round_ + 1)]):
@@ -245,19 +244,15 @@ def tile_aftblock_pa_kernel(tc, z_current, z_window, Wq, Wk, Wv, Wo, out):
                     row_maxima(first_steps)
                 if round_ == first_known + 1:
                     negated_maximum(spread_first, first_steps)
-                on_vector = (PAIR,) if round_ >= wo_rounds else ()
-                flipped_groups = [(transpose_group(blocks, on_vector), codes, scales) for blocks, codes, scales in later[round_]]
+                flipped_groups = [(transpose_group(blocks), codes, scales) for blocks, codes, scales in later[round_]]
                 if round_ < wo_rounds:
                     waiting = flipped_groups
                 else:
                     wo_waiting += flipped_groups
                 if round_ == first_known:
                     spread_first = spread_maxima(first_steps)
-                if round_ >= wo_rounds - 2:
-                    count = exps[round_ - wo_rounds + 2]
-                    for c, w in early[early_done : early_done + count]:
-                        exponential(c, w)
-                    early_done += count
+                if round_ >= EARLY_ROUND:
+                    exponential(*early[round_ - EARLY_ROUND])
 
             row_maxima(last_steps)
             ahead = [v_pass(0, w) for w in range(2)]

@@ -24,7 +24,7 @@ WORDS = L // 2
 GROUP = 4
 PAIR = 2
 EARLY_ROUND = 10
-GATE_LAG = 3
+GATE_LAG = 2
 ROUND = 2
 RUN = 4
 GPSIMD_STEPS = (6, 6, 5, 3)
@@ -136,6 +136,14 @@ def tile_aftblock_pa_kernel(tc, z_current, z_window, Wq, Wk, Wv, Wo, out):
             for g in range(CHUNKS):
                 load_wo(g)
 
+            def halves(block):
+                return [block[:, u:WORDS:2] for u in range(2)]
+
+            def permute(block):
+                permuted = stage.tile([P, 2, P], F32, name="permuted")
+                nc.scalar.copy(out=permuted[:], in_=block.rearrange("p (i u) -> p u i", u=2))
+                return [permuted[:, u, :] for u in range(2)]
+
             def transpose_group(blocks, on_vector=()):
                 grouped = stage.tile([P, len(blocks) * P * BLOCKS], BF16, name="grouped", align_bytes=64)
                 words = grouped[:].bitcast(F32).rearrange("p (k r u) -> p k r u", r=P, u=2)
@@ -144,7 +152,7 @@ def tile_aftblock_pa_kernel(tc, z_current, z_window, Wq, Wk, Wv, Wo, out):
                     flipped = flip.tile([P, PAIR, 2, P], F32, name="flipped")
                     for k, block in enumerate(pair):
                         for u in range(2):
-                            nc.tensor.transpose(flipped[:, k, u, :], block[:, u : WORDS : 2], ident[:])
+                            nc.tensor.transpose(flipped[:, k, u, :], block[u], ident[:])
                     source = flipped[:, 0 : len(pair)].rearrange("p k u r -> p k r u")
                     target = words[:, first : first + len(pair)]
                     if first in on_vector:
@@ -163,12 +171,12 @@ def tile_aftblock_pa_kernel(tc, z_current, z_window, Wq, Wk, Wv, Wo, out):
             def group_of(blocks, codes, scales, i):
                 return piece(blocks, codes, scales, GROUP * i, GROUP)
 
-            z_blocks = [z_raw[:, s, :].bitcast(F32) for s in range(W + 1)]
-            wk_blocks = [wk_raw[:, j, :].bitcast(F32) for j in range(A // P)]
-            wv_blocks = [wv_raw[:, j, :].bitcast(F32) for j in range(A // P)]
-            wq_blocks = [wq_raw[:, j, :].bitcast(F32) for j in range(A // P)]
+            z_blocks = [halves(z_raw[:, s, :].bitcast(F32)) for s in range(W + 1)]
+            wk_blocks = [halves(wk_raw[:, j, :].bitcast(F32)) for j in range(A // P)]
+            wv_blocks = [halves(wv_raw[:, j, :].bitcast(F32)) for j in range(A // P)]
+            wq_blocks = [halves(wq_raw[:, j, :].bitcast(F32)) for j in range(A // P)]
             wo_blocks = [
-                wo_raw[:, i, :].bitcast(F32)[:, WORDS * g : WORDS * (g + 1)]
+                halves(wo_raw[:, i, :].bitcast(F32)[:, WORDS * g : WORDS * (g + 1)])
                 for g in range(CHUNKS)
                 for i in range(L // P)
             ]
@@ -227,6 +235,13 @@ def tile_aftblock_pa_kernel(tc, z_current, z_window, Wq, Wk, Wv, Wo, out):
             first_known = rounds // 2
             early = [(c, w) for c in range(CHUNKS) for w in range(BLOCKS)][: rounds - EARLY_ROUND]
             wo_waiting = []
+            raw_pairs = {3: [z_raw[:, GROUP + k, :] for k in range(PAIR)]}
+            for c in range(1, CHUNKS):
+                raw_pairs[c - 1] = [wk_raw[:, BLOCKS * c + k, :] for k in range(PAIR)]
+            for c in range(CHUNKS):
+                raw_pairs[CHUNKS + c] = [wq_raw[:, BLOCKS * c + k, :] for k in range(PAIR)]
+                raw_pairs[2 * CHUNKS + c] = [wv_raw[:, BLOCKS * c + k, :] for k in range(PAIR)]
+            permuted_pairs = {}
             for round_ in range(rounds):
                 for n, (c, w) in enumerate(k_order[ROUND * round_ : ROUND * (round_ + 1)]):
                     k_ps = banks.tile([P, CHUNK], F32, name="k_ps", tag="bank")
@@ -244,7 +259,13 @@ def tile_aftblock_pa_kernel(tc, z_current, z_window, Wq, Wk, Wv, Wo, out):
                     row_maxima(first_steps)
                 if round_ == first_known + 1:
                     negated_maximum(spread_first, first_steps)
-                flipped_groups = [(transpose_group(blocks), codes, scales) for blocks, codes, scales in later[round_]]
+                flipped_groups = []
+                ready_pair = permuted_pairs.get(round_, [])
+                for blocks, codes, scales in later[round_]:
+                    flipped_groups.append((transpose_group(ready_pair + blocks[len(ready_pair) :]), codes, scales))
+                    ready_pair = []
+                if round_ < 9:
+                    permuted_pairs[round_ + 2] = [permute(block.bitcast(F32)) for block in raw_pairs[round_ + 2]]
                 if round_ < wo_rounds:
                     waiting = flipped_groups
                 else:

from contextlib import ExitStack

import concourse.mybir as mybir
from concourse.masks import make_identity

F32 = mybir.dt.float32
BF16 = mybir.dt.bfloat16
U32 = mybir.dt.uint32
U8 = mybir.dt.uint8
FP8X4 = mybir.dt.float8_e4m3fn_x4
ALU = mybir.AluOpType
ACT = mybir.ActivationFunctionType
AXIS_X = mybir.AxisListType.X

P = 128
L = 512
A = 2048
W = 8
EPS = 1e-8
CHUNK = 512
CHUNKS = A // CHUNK
BLOCKS = CHUNK // P
WORDS = L // 2
GROUP = 4
PAIR = 2
EARLY_ROUND = 10
GATE_LAG = 2
ROUND = 2
RUN = 4
GPSIMD_STEPS = (6, 6, 5, 3)

FLOPS = 2 * P * L * A * (1 + 2 * W) + 2 * P * A * L


def tile_aftblock_pa_kernel(tc, z_current, z_window, Wq, Wk, Wv, Wo, out):
    nc = tc.nc
    with ExitStack() as ctx:
        ctx.enter_context(tc.manual_schedule())
        keep = ctx.enter_context(tc.tile_pool(name="keep", bufs=1))
        stage = ctx.enter_context(tc.tile_pool(name="stage", bufs=6))
        banks = ctx.enter_context(tc.psum_pool(name="banks", bufs=4))

        ident = keep.tile([P, P], F32, name="ident")
        make_identity(nc, ident[:])

        z_codes = keep.tile([P, (W + 1) * P], U32, name="z_codes", align_bytes=64)
        z_scales = keep.tile([P, (W + 1) * P], U8, name="z_scales", align_bytes=64)
        wk_codes = keep.tile([P, A], U32, name="wk_codes", align_bytes=64)
        wk_scales = keep.tile([P, A], U8, name="wk_scales", align_bytes=64)
        wv_codes = keep.tile([P, A], U32, name="wv_codes", align_bytes=64)
        wv_scales = keep.tile([P, A], U8, name="wv_scales", align_bytes=64)
        wq_codes = keep.tile([P, A], U32, name="wq_codes", align_bytes=64)
        wq_scales = keep.tile([P, A], U8, name="wq_scales", align_bytes=64)
        wo_codes = keep.tile([P, CHUNKS * L], U32, name="wo_codes", align_bytes=64)
        wo_scales = keep.tile([P, CHUNKS * L], U8, name="wo_scales", align_bytes=64)

        k_sb = keep.tile([P, CHUNKS, W, CHUNK], F32, name="k_sb")
        bank_max = keep.tile([P, CHUNKS, W], F32, name="bank_max")
        row_max = keep.tile([P, W], F32, name="row_max")
        neg_m = keep.tile([P, W], F32, name="neg_m")
        gate = keep.tile([P, CHUNKS, P, BLOCKS], F32, name="gate")
        partial = keep.tile([P, CHUNKS, CHUNK], F32, name="partial")

        def mx_pass(acc, lhs_codes, lhs_scales, lhs_cols, rhs_codes, rhs_scales, rhs_cols, start, stop):
            nc.tensor.matmul_mx(
                out=acc,
                lhsT=lhs_codes[:, lhs_cols].bitcast(FP8X4),
                lhsT_scale=lhs_scales[:, lhs_cols],
                rhs=rhs_codes[:, rhs_cols].bitcast(FP8X4),
                rhs_scale=rhs_scales[:, rhs_cols],
                start=start,
                stop=stop,
            )

        def step_cols(w):
            return slice(w * P, (w + 1) * P)

        def chunk_cols(c):
            return slice(c * CHUNK, (c + 1) * CHUNK)

        def exponential(c, w):
            e = k_sb[:, c, w, :]
            nc.scalar.activation(out=e, in_=e, func=ACT.Exp, bias=neg_m[:, w : w + 1], scale=1.0)
            if w == 1:
                nc.gpsimd.tensor_tensor(out=partial[:, c, :], in0=k_sb[:, c, 0, :], in1=e, op=ALU.add)
            elif 1 < w < GPSIMD_STEPS[c]:
                nc.gpsimd.tensor_tensor(out=partial[:, c, :], in0=partial[:, c, :], in1=e, op=ALU.add)

        def v_pass(c, w):
            v_ps = banks.tile([P, CHUNK], F32, name="v_ps", tag="bank")
            mx_pass(v_ps[:], z_codes, z_scales, step_cols(w), wv_codes, wv_scales, chunk_cols(c), True, True)
            return v_ps

        with tc.tile_pool(name="raw", bufs=1) as raw, tc.psum_pool(name="flip", bufs=4) as flip:
            z_raw = raw.tile([P, W + 1, L], BF16, name="z_raw")
            wk_raw = raw.tile([P, A // P, L], BF16, name="wk_raw")
            wv_raw = raw.tile([P, A // P, L], BF16, name="wv_raw")
            wq_raw = raw.tile([P, A // P, L], BF16, name="wq_raw")
            wo_raw = raw.tile([P, L // P, A], BF16, name="wo_raw")

            def load_steps(first, count):
                steps = slice(first, first + count)
                nc.sync.dma_start(out=z_raw[:, steps, :], in_=z_window[steps].rearrange("w b l -> b w l"))

            def load_features(tile_, weight, c, first=0, count=BLOCKS):
                rows = weight.rearrange("(c r t) l -> r c t l", c=CHUNKS, t=BLOCKS)
                start = BLOCKS * c + first
                nc.sync.dma_start(out=tile_[:, start : start + count, :], in_=rows[:, c, first : first + count])

            def load_wo(g):
                nc.sync.dma_start(out=wo_raw[:, :, chunk_cols(g)], in_=Wo.rearrange("(i p) a -> p i a", p=P)[:, :, chunk_cols(g)])

            zeros = keep.tile([P, CHUNK], BF16, name="zeros")
            nc.vector.memset(zeros[:], 0.0)

            def warm_up(count):
                for n in range(count):
                    dummy = banks.tile([P, CHUNK], F32, name="dummy", tag="bank")
                    nc.tensor.matmul(out=dummy[:], lhsT=zeros[:, :P], rhs=zeros[:], start=True, stop=True)

            warm_up(2)

            load_steps(0, PAIR)
            load_features(wk_raw, Wk, 0, 0, PAIR)
            for first in range(PAIR, BLOCKS):
                load_features(wk_raw, Wk, 0, first, 1)
            load_steps(PAIR, PAIR)
            for c in range(1, CHUNKS):
                load_features(wk_raw, Wk, c)
            load_steps(GROUP, GROUP)
            nc.sync.dma_start(out=z_raw[:, W, :], in_=z_current)
            for c in range(CHUNKS):
                load_features(wq_raw, Wq, c)
            for c in range(CHUNKS):
                load_features(wv_raw, Wv, c)
            for g in range(CHUNKS):
                load_wo(g)

            def halves(block):
                return [block[:, u:WORDS:2] for u in range(2)]

            def permute(block):
                permuted = stage.tile([P, 2, P], F32, name="permuted")
                nc.scalar.copy(out=permuted[:], in_=block.rearrange("p (i u) -> p u i", u=2))
                return [permuted[:, u, :] for u in range(2)]

            def transpose_group(blocks, on_vector=()):
                grouped = stage.tile([P, len(blocks) * P * BLOCKS], BF16, name="grouped", align_bytes=64)
                words = grouped[:].bitcast(F32).rearrange("p (k r u) -> p k r u", r=P, u=2)
                for first in range(0, len(blocks), PAIR):
                    pair = blocks[first : first + PAIR]
                    flipped = flip.tile([P, PAIR, 2, P], F32, name="flipped")
                    for k, block in enumerate(pair):
                        for u in range(2):
                            nc.tensor.transpose(flipped[:, k, u, :], block[u], ident[:])
                    source = flipped[:, 0 : len(pair)].rearrange("p k u r -> p k r u")
                    target = words[:, first : first + len(pair)]
                    if first in on_vector:
                        nc.vector.tensor_copy(out=target, in_=source)
                    else:
                        nc.scalar.copy(out=target, in_=source)
                return grouped

            def quantise(grouped, codes, scales):
                nc.vector.quantize_mx(out=codes.bitcast(FP8X4), scales=scales, in_=grouped[:])

            def piece(blocks, codes, scales, first, count):
                cols = slice(P * first, P * (first + count))
                return blocks[first : first + count], codes[:, cols], scales[:, cols]

            def group_of(blocks, codes, scales, i):
                return piece(blocks, codes, scales, GROUP * i, GROUP)

            z_blocks = [halves(z_raw[:, s, :].bitcast(F32)) for s in range(W + 1)]
            wk_blocks = [halves(wk_raw[:, j, :].bitcast(F32)) for j in range(A // P)]
            wv_blocks = [halves(wv_raw[:, j, :].bitcast(F32)) for j in range(A // P)]
            wq_blocks = [halves(wq_raw[:, j, :].bitcast(F32)) for j in range(A // P)]
            wo_blocks = [
                halves(wo_raw[:, i, :].bitcast(F32)[:, WORDS * g : WORDS * (g + 1)])
                for g in range(CHUNKS)
                for i in range(L // P)
            ]

            head = [
                piece(z_blocks, z_codes, z_scales, 0, PAIR),
                piece(wk_blocks, wk_codes, wk_scales, 0, PAIR),
                piece(wk_blocks, wk_codes, wk_scales, PAIR, 1),
                piece(wk_blocks, wk_codes, wk_scales, PAIR + 1, 1),
                piece(z_blocks, z_codes, z_scales, PAIR, PAIR),
            ]
            waiting = []
            for i, (blocks, codes, scales) in enumerate(head):
                waiting.append((transpose_group(blocks, (0,) if i == 1 else ()), codes, scales))
            for ready in waiting[:-1]:
                quantise(*ready)
            waiting = waiting[-1:]

            later = (
                [[group_of(wk_blocks, wk_codes, wk_scales, c)] for c in range(1, CHUNKS)]
                + [[group_of(z_blocks, z_codes, z_scales, 1), piece(z_blocks, z_codes, z_scales, W, 1)]]
                + [[group_of(wq_blocks, wq_codes, wq_scales, c)] for c in range(CHUNKS)]
                + [[group_of(wv_blocks, wv_codes, wv_scales, c)] for c in range(CHUNKS)]
            )
            wo_rounds = len(later)
            later += [[group_of(wo_blocks, wo_codes, wo_scales, g)] for g in range(CHUNKS)]

            def gate_chunk(c):
                q_ps = flip.tile([P, BLOCKS, P], F32, name="q_ps", tag="flipped")
                for t in range(BLOCKS):
                    mx_pass(q_ps[:, t, :], wq_codes, wq_scales, step_cols(BLOCKS * c + t),
                            z_codes, z_scales, step_cols(W), True, True)
                nc.scalar.activation(out=gate[:, c], in_=q_ps[:].rearrange("p t b -> p b t"), func=ACT.Exp, scale=-1.0)
                flat = gate[:, c].rearrange("p b t -> p (b t)")
                nc.gpsimd.tensor_scalar(out=flat, in0=flat, scalar1=1.0, scalar2=1.0, op0=ALU.add, op1=ALU.mult)

            def row_maxima(first):
                steps = slice(first, first + BLOCKS)
                nc.vector.tensor_reduce(
                    out=row_max[:, steps], in_=bank_max[:, :, steps].rearrange("p c w -> p w c"), axis=AXIS_X, op=ALU.max
                )

            def spread_maxima(first):
                spread = flip.tile([P, BLOCKS, P], F32, name="spread", tag="flipped")
                for i in range(BLOCKS):
                    nc.tensor.transpose(spread[:, i, :], row_max[:, first + i : first + i + 1].to_broadcast([P, P]), ident[:])
                return spread

            def negated_maximum(spread, first):
                nc.vector.tensor_reduce(out=neg_m[:, first : first + BLOCKS], in_=spread[:], axis=AXIS_X, op=ALU.max, negate=True)

            first_steps = 0
            last_steps = BLOCKS
            k_order = [(c, w) for first in (first_steps, last_steps) for c in range(CHUNKS) for w in range(first, first + BLOCKS)]
            rounds = len(later)
            first_known = rounds // 2
            early = [(c, w) for c in range(CHUNKS) for w in range(BLOCKS)][: rounds - EARLY_ROUND]
            wo_waiting = []
            raw_pairs = {3: [z_raw[:, GROUP + k, :] for k in range(PAIR)]}
            for c in range(1, CHUNKS):
                raw_pairs[c - 1] = [wk_raw[:, BLOCKS * c + k, :] for k in range(PAIR)]
            for c in range(CHUNKS):
                raw_pairs[CHUNKS + c] = [wq_raw[:, BLOCKS * c + k, :] for k in range(PAIR)]
                raw_pairs[2 * CHUNKS + c] = [wv_raw[:, BLOCKS * c + k, :] for k in range(PAIR)]
            permuted_pairs = {}
            for round_ in range(rounds):
                for n, (c, w) in enumerate(k_order[ROUND * round_ : ROUND * (round_ + 1)]):
                    k_ps = banks.tile([P, CHUNK], F32, name="k_ps", tag="bank")
                    mx_pass(k_ps[:], z_codes, z_scales, step_cols(w), wk_codes, wk_scales, chunk_cols(c), True, True)
                    nc.vector.tensor_scalar(
                        out=k_sb[:, c, w, :], in0=k_ps[:], scalar1=1.0, scalar2=None,
                        op0=ALU.mult, op1=ALU.max, accum_out=bank_max[:, c, w : w + 1],
                    )
                    for ready in waiting:
                        quantise(*ready)
                    waiting = []
                if 0 <= round_ - CHUNKS - GATE_LAG < CHUNKS:
                    gate_chunk(round_ - CHUNKS - GATE_LAG)
                if round_ == first_known - 1:
                    row_maxima(first_steps)
                if round_ == first_known + 1:
                    negated_maximum(spread_first, first_steps)
                flipped_groups = []
                ready_pair = permuted_pairs.get(round_, [])
                for blocks, codes, scales in later[round_]:
                    flipped_groups.append((transpose_group(ready_pair + blocks[len(ready_pair) :]), codes, scales))
                    ready_pair = []
                if round_ < 9:
                    permuted_pairs[round_ + 2] = [permute(block.bitcast(F32)) for block in raw_pairs[round_ + 2]]
                if round_ < wo_rounds:
                    waiting = flipped_groups
                else:
                    wo_waiting += flipped_groups
                if round_ == first_known:
                    spread_first = spread_maxima(first_steps)
                if round_ >= EARLY_ROUND:
                    exponential(*early[round_ - EARLY_ROUND])

            row_maxima(last_steps)
            ahead = [v_pass(0, w) for w in range(2)]
            spread_last = spread_maxima(last_steps)
            quantise(*wo_waiting[0])
            negated_maximum(spread_last, last_steps)
            for c in range(CHUNKS):
                for w in range(W):
                    if (c, w) not in early:
                        exponential(c, w)

        with tc.tile_pool(name="prod", bufs=3 * RUN) as prod, tc.tile_pool(name="small", bufs=2) as small, tc.tile_pool(
            name="late", bufs=1
        ) as late, tc.psum_pool(name="sums", bufs=CHUNKS - 1) as sums, tc.psum_pool(name="dens", bufs=1) as dens:
            divisor = late.tile([P, CHUNKS, P, BLOCKS], F32, name="divisor")
            h_codes = late.tile([P, CHUNKS, P], U32, name="h_codes", align_bytes=64)
            h_scales = late.tile([P, CHUNKS, P], U8, name="h_scales", align_bytes=64)
            out_sb = late.tile([P, L], F32, name="out_sb")
            products = {}
            numerator = {}

            def add_transposed(bank, source, first, last):
                for t in range(BLOCKS):
                    nc.tensor.matmul(
                        out=bank[:, t, :], lhsT=source[:, P * t : P * (t + 1)], rhs=ident[:], is_transpose=True,
                        start=first and t == 0, stop=last and t == BLOCKS - 1,
                    )

            def multiply(c, w, v_ps):
                ev = prod.tile([P, CHUNK], F32, name="ev")
                nc.vector.tensor_tensor(out=ev[:], in0=k_sb[:, c, w, :], in1=v_ps[:], op=ALU.mult)
                products[(c, w)] = ev

            def sum_products(c, steps):
                if c not in numerator:
                    numerator[c] = sums.tile([P, BLOCKS, P], F32, name="sum_ps")
                for w in steps:
                    add_transposed(numerator[c], products[(c, w)], w == 0, w == W - 1)

            def denominator(c):
                den_ps = dens.tile([P, BLOCKS, P], F32, name="den_ps")
                add_transposed(den_ps, partial[:, c, :], True, False)
                for w in range(GPSIMD_STEPS[c], W):
                    add_transposed(den_ps, k_sb[:, c, w, :], False, w == W - 1)
                return den_ps

            def reciprocal_divisor(c, den_ps):
                nc.vector.scalar_tensor_tensor(
                    out=divisor[:, c], in0=den_ps[:].rearrange("p t b -> p b t"), scalar=EPS, in1=gate[:, c],
                    op0=ALU.add, op1=ALU.mult,
                )
                nc.scalar.activation(out=divisor[:, c], in_=divisor[:, c], func=ACT.Abs_reciprocal_sqrt)
                nc.scalar.activation(out=divisor[:, c], in_=divisor[:, c], func=ACT.Square)

            def hidden(c):
                h = small.tile([P, P, BLOCKS], BF16, name="h", align_bytes=64)
                nc.vector.tensor_tensor(out=h[:], in0=numerator[c][:].rearrange("p t b -> p b t"), in1=divisor[:, c], op=ALU.mult)
                nc.vector.quantize_mx(out=h_codes[:, c, :].bitcast(FP8X4), scales=h_scales[:, c, :],
                                      in_=h[:].rearrange("p b t -> p (b t)"))

            runs = [(c, range(first, first + RUN)) for c in range(CHUNKS) for first in range(0, W, RUN)]
            last_run = len(runs) - 1
            den_runs = {2: 0, 4: 1, 5: 2, 6: 3}
            hidden_after = {6: 0, 7: 2}
            hidden_in = {7: 1}
            for i, (c, steps) in enumerate(runs):
                for n, w in enumerate(steps):
                    multiply(c, w, ahead.pop(0) if ahead else v_pass(c, w))
                    if n == 0 and i - 1 in den_runs:
                        reciprocal_divisor(den_runs[i - 1], den_ps)
                    if n == 1 and i in hidden_in:
                        hidden(hidden_in[i])
                if i >= 1:
                    sum_products(*runs[i - 1])
                if i in den_runs:
                    den_ps = denominator(den_runs[i])
                if last_run - CHUNKS < i < last_run:
                    quantise(*wo_waiting[i - last_run + CHUNKS])
                if i in hidden_after:
                    hidden(hidden_after[i])
            sum_products(*runs[-1])
            hidden(CHUNKS - 1)

            half_l = L // 2
            out_ps = [banks.tile([P, half_l], F32, name="out_ps%d" % s, tag="bank") for s in range(2)]
            for c in range(CHUNKS):
                for s in range(2):
                    cols = slice(c * L + s * half_l, c * L + (s + 1) * half_l)
                    nc.tensor.matmul_mx(
                        out=out_ps[s][:], lhsT=h_codes[:, c, :].bitcast(FP8X4), lhsT_scale=h_scales[:, c, :],
                        rhs=wo_codes[:, cols].bitcast(FP8X4), rhs_scale=wo_scales[:, cols],
                        start=c == 0, stop=c == CHUNKS - 1,
                    )
            nc.scalar.copy(out=out_sb[:, :half_l], in_=out_ps[0][:])
            nc.scalar.dma_start(out=out[:, :half_l], in_=out_sb[:, :half_l])
            nc.vector.tensor_copy(out=out_sb[:, half_l:], in_=out_ps[1][:])
            nc.sync.dma_start(out=out[:, half_l:], in_=out_sb[:, half_l:])
